import numpy as np
import ml_dtypes


def mxq(x, axis, fmt="e4m3"):
    dtype, down = {"e4m3": (ml_dtypes.float8_e4m3fn, 7), "e5m2": (ml_dtypes.float8_e5m2, 14)}[fmt]
    v = np.moveaxis(np.asarray(x, np.float32).astype(ml_dtypes.bfloat16).astype(np.float64), axis, -1)
    blocks = v.reshape(v.shape[:-1] + (-1, 32))
    amax = np.abs(blocks).max(-1, keepdims=True)
    byte = np.maximum(np.where(amax > 0, np.frexp(amax)[1] - 1 + 127, 0) - down, 1)
    scale = np.exp2(byte - 127.0)
    codes = (blocks / scale).astype(np.float32).astype(dtype).astype(np.float64)
    return np.moveaxis((codes * scale).reshape(v.shape), -1, axis)


WIDE = False


def mx_kscale(k):
    if not WIDE:
        return np.ones(k)
    levels = np.array([10, -10, 5, -5, 0])
    a = np.random.permutation(np.resize(levels, k // 512 * 4)).reshape(k // 512, 4)
    idx = np.arange(k)
    return np.exp2(a[idx // 512, idx % 128 // 32])


BF16 = ml_dtypes.bfloat16


def bf(x):
    return np.asarray(x, np.float32).astype(BF16)


def f64(x):
    return np.asarray(x).astype(np.float64)


N, M, K = 6, 512, 128
DIM = 1
DROP_P = 0.1


def setup_inputs():
    s = mx_kscale(M)
    r = s / s.max()
    x1 = np.random.standard_normal((1, N, M, K)) * np.sqrt(2.5) / K ** 0.25 * r[None, None, :, None]
    u = np.random.random((N, N, M, M))
    dropout_mask = (u >= DROP_P).astype(np.float64) / (1.0 - DROP_P) / r[None, None, None, :]
    return {"x1": bf(x1), "dropout_mask": bf(dropout_mask)}


def reference(x1, dropout_mask):
    x = f64(x1)
    scale = np.sqrt(DIM)
    key_t = x.transpose(1, 0, 2, 3)
    qk = x @ key_t.swapaxes(-2, -1)
    z = qk * scale
    e = np.exp(z - z.max(-1, keepdims=True))
    attn = e / e.sum(-1, keepdims=True)
    dropped = attn * f64(dropout_mask)
    return mxq(dropped, 3, "e4m3") @ mxq(x, 2, "e4m3")

@@ -1,0 +1,243 @@
+from contextlib import ExitStack
+
+import concourse.mybir as mybir
+from concourse.masks import make_identity
+
+F32 = mybir.dt.float32
+BF16 = mybir.dt.bfloat16
+U32 = mybir.dt.uint32
+U8 = mybir.dt.uint8
+FP8X4 = mybir.dt.float8_e4m3fn_x4
+ACT = mybir.ActivationFunctionType
+ALU = mybir.AluOpType
+AX = mybir.AxisListType
+
+NG = 6
+ROWS = 512
+D = 128
+P = 128
+MT = 4
+FLOPS = 2 * 2 * NG * NG * ROWS * ROWS * D
+
+PIN = False
+PF = 8
+OC_V_EVERY = 0
+
+
+def tile_model_kernel(tc, x1, dropout_mask, out):
+    nc = tc.nc
+    pairs = [(i, j) for i in range(NG) for j in range(NG)]
+    npairs = len(pairs)
+    with ExitStack() as ctx:
+        const = ctx.enter_context(tc.tile_pool(name="const", bufs=1))
+        mpool = ctx.enter_context(tc.tile_pool(name="mask", bufs=PF))
+        epool = ctx.enter_context(tc.tile_pool(name="expo", bufs=10))
+        dpool = ctx.enter_context(tc.tile_pool(name="drop", bufs=8))
+        gpool = ctx.enter_context(tc.tile_pool(name="grouped", bufs=3))
+        qpool = ctx.enter_context(tc.tile_pool(name="quant", bufs=3))
+        opool = ctx.enter_context(tc.tile_pool(name="outs", bufs=3))
+        spool = ctx.enter_context(tc.tile_pool(name="stats", bufs=4))
+        gps = ctx.enter_context(tc.psum_pool(name="gps", bufs=5))
+        tps = ctx.enter_context(tc.psum_pool(name="tps", bufs=2))
+        ops = ctx.enter_context(tc.psum_pool(name="ops", bufs=1))
+
+        warm = const.tile([P, 1], F32, name="warm")
+        warm2 = const.tile([P, 1], F32, name="warm2")
+        nc.vector.memset(warm[:], 0.0)
+        nc.scalar.activation(out=warm2[:], in_=warm[:], func=ACT.Exp)
+
+        ident = const.tile([P, P], BF16, name="ident")
+        make_identity(nc, ident[:])
+
+        xa = const.tile([P, NG, MT, D], BF16, name="xa")
+        xc = const.tile([P, NG, MT, D], BF16, name="xc")
+        xtm = const.tile([P, NG, MT, P], BF16, name="xtm")
+        xtn = const.tile([P, NG, MT, P], BF16, name="xtn")
+        xg = const.tile([P, NG, D, MT], BF16, name="xg", align_bytes=64)
+        xq = const.tile([P, NG * D], U32, name="xq", align_bytes=64)
+        xs = const.tile([P, NG * D], U8, name="xs", align_bytes=64)
+
+        mk = {}
+        nmax = {}
+        ssum = {}
+        rs = {}
+        et = {}
+        xt = {}
+        grp = {}
+
+        def load(q):
+            i, j = pairs[q]
+            m = mpool.tile([P, MT, ROWS], BF16, name="mk")
+            nc.sync.dma_start(
+                out=m[:], in_=dropout_mask[i, j].rearrange("(p t) n -> p t n", t=MT)
+            )
+            mk[q] = m
+
+        def setup_m(j):
+            st = gps.tile([P, MT, P], BF16, tag="g", name="stm")
+            for t in range(MT):
+                nc.tensor.transpose(st[:, t, :], xa[:, j, t, :], ident[:])
+            nc.vector.tensor_scalar_mul(out=xtm[:, j], in0=st[:], scalar1=-1.0)
+
+        def setup_n(i):
+            st = gps.tile([P, MT, P], BF16, tag="g", name="stn")
+            for c in range(MT):
+                nc.tensor.transpose(st[:, c, :], xc[:, i, c, :], ident[:])
+            nc.scalar.copy(out=xtn[:, i], in_=st[:])
+
+        def stage_a(q, t):
+            i, j = pairs[q]
+            if t == 0:
+                nmax[q] = spool.tile([P, MT], F32, name="nmax")
+                ssum[q] = spool.tile([P, MT], F32, name="ssum")
+            g = gps.tile([P, ROWS], F32, tag="g", name="g")
+            nc.tensor.matmul(
+                out=g[:],
+                lhsT=xtm[:, j, t, :],
+                rhs=xtn[:, i].rearrange("k c p -> k (c p)"),
+                start=True,
+                stop=True,
+            )
+            nc.vector.tensor_reduce(
+                out=nmax[q][:, t : t + 1], in_=g[:], axis=AX.X, op=ALU.min
+            )
+            e = epool.tile([P, ROWS], F32, name="e")
+            nc.scalar.activation(
+                out=e[:],
+                in_=g[:],
+                func=ACT.Exp,
+                bias=nmax[q][:, t : t + 1],
+                scale=-1.0,
+                accum_out=ssum[q][:, t : t + 1],
+            )
+            et[(q, t)] = e
+
+        def recip(q):
+            rs[q] = spool.tile([P, MT], F32, name="rs")
+            nc.vector.reciprocal(out=rs[q][:], in_=ssum[q][:])
+
+        def stage_b(q, t):
+            d = dpool.tile([P, ROWS], BF16, name="d")
+            nc.vector.scalar_tensor_tensor(
+                out=d[:],
+                in0=et[(q, t)][:],
+                scalar=rs[q][:, t : t + 1],
+                in1=mk[q][:, t, :],
+                op0=ALU.mult,
+                op1=ALU.mult,
+            )
+            h, a = divmod(t, 2)
+            if a == 0:
+                xt[(q, h)] = tps.tile([P, 2, MT, P], BF16, name="xt")
+            for c in range(MT):
+                nc.tensor.transpose(
+                    xt[(q, h)][:, a, c, :], d[:, c * P : (c + 1) * P], ident[:]
+                )
+
+        def cpy(q, h):
+            if h == 0:
+                grp[q] = gpool.tile([P, ROWS, MT], BF16, name="grp", align_bytes=64)
+            nc.scalar.copy(
+                out=grp[q][:, h * 2 * P : (h + 1) * 2 * P, :].rearrange(
+                    "p (a m) c -> p a m c", a=2
+                ),
+                in_=xt[(q, h)][:].rearrange("p a c m -> p a m c"),
+            )
+
+        def quant_x():
+            flat = xg[:].rearrange("p j k c -> p (j k c)")
+            nc.vector.quantize_mx(
+                out=xq[:, 0:512].bitcast(FP8X4), scales=xs[:, 0:512], in_=flat[:, 0:2048]
+            )
+            nc.vector.quantize_mx(
+                out=xq[:, 512:768].bitcast(FP8X4),
+                scales=xs[:, 512:768],
+                in_=flat[:, 2048:3072],
+            )
+
+        def stage_c(q):
+            i, j = pairs[q]
+            codes = qpool.tile([P, ROWS], U32, name="codes", align_bytes=64)
+            scl = qpool.tile([P, ROWS], U8, name="scl", align_bytes=64)
+            nc.vector.quantize_mx(
+                out=codes[:].bitcast(FP8X4),
+                scales=scl[:],
+                in_=grp[q][:].rearrange("p m c -> p (m c)"),
+            )
+            o = ops.tile([P, MT, D], F32, name="o")
+            for t in range(MT):
+                nc.tensor.matmul_mx(
+                    out=o[:, t, :],
+                    lhsT=codes[:, t * P : (t + 1) * P].bitcast(FP8X4),
+                    lhsT_scale=scl[:, t * P : (t + 1) * P],
+                    rhs=xq[:, j * D : (j + 1) * D].bitcast(FP8X4),
+                    rhs_scale=xs[:, j * D : (j + 1) * D],
+                    start=True,
+                    stop=True,
+                )
+            ob = opool.tile([P, MT, D], F32, name="ob")
+            if OC_V_EVERY > 0 and q % OC_V_EVERY == 0:
+                nc.vector.tensor_copy(out=ob[:], in_=o[:])
+            else:
+                nc.scalar.copy(out=ob[:], in_=o[:])
+            nc.sync.dma_start(
+                out=out[i, j].rearrange("(p t) k -> p t k", t=MT), in_=ob[:]
+            )
+
+        nc.sync.dma_start(
+            out=xa[:, 0], in_=x1[0, 0].rearrange("(p t) k -> p t k", t=MT)
+        )
+        nc.sync.dma_start(
+            out=xc[:, 0], in_=x1[0, 0].rearrange("(c p) k -> p c k", p=P)
+        )
+        load(0)
+        nc.sync.dma_start(
+            out=xa[:, 1:], in_=x1[0, 1:].rearrange("j (p t) k -> p j t k", t=MT)
+        )
+        nc.sync.dma_start(
+            out=xc[:, 1:], in_=x1[0, 1:].rearrange("j (c p) k -> p j c k", p=P)
+        )
+        for q in range(1, PF):
+            load(q)
+
+        if PIN:
+            ctx.enter_context(tc.manual_schedule())
+
+        setup_n(0)
+        setup_m(0)
+        for t in range(MT):
+            stage_a(0, t)
+        nc.gpsimd.tensor_scalar(
+            out=xg[:],
+            in0=xc[:].rearrange("p j c k -> p j k c"),
+            scalar1=1.0,
+            scalar2=0.0,
+            op0=ALU.mult,
+            op1=ALU.add,
+        )
+
+        for q in range(npairs):
+            nq = q + 1
+            if nq < npairs:
+                ni, nj = pairs[nq]
+                if ni == 0:
+                    setup_m(nj)
+                elif nj == 0:
+                    setup_n(ni)
+            for t in range(MT):
+                if nq < npairs:
+                    stage_a(nq, t)
+                if t == 0:
+                    recip(q)
+                stage_b(q, t)
+                if t == 1:
+                    cpy(q, 0)
+                    if q == 1:
+                        quant_x()
+                    if q >= 1:
+                        stage_c(q - 1)
+                if t == 3:
+                    cpy(q, 1)
+            if q + PF < npairs:
+                load(q + PF)
+        stage_c(npairs - 1)

@@ -19,24 +19,27 @@ P = 128
 MT = 4
 FLOPS = 2 * 2 * NG * NG * ROWS * ROWS * D
 
-PIN = False
+PIN = True
 PF = 8
-OC_V_EVERY = 0
+LEAD = 6
+OCV = 0
 
 
 def tile_model_kernel(tc, x1, dropout_mask, out):
     nc = tc.nc
     pairs = [(i, j) for i in range(NG) for j in range(NG)]
     npairs = len(pairs)
+    ntiles = npairs * MT
+    nbanks = npairs * 2
     with ExitStack() as ctx:
         const = ctx.enter_context(tc.tile_pool(name="const", bufs=1))
         mpool = ctx.enter_context(tc.tile_pool(name="mask", bufs=PF))
-        epool = ctx.enter_context(tc.tile_pool(name="expo", bufs=10))
-        dpool = ctx.enter_context(tc.tile_pool(name="drop", bufs=8))
-        gpool = ctx.enter_context(tc.tile_pool(name="grouped", bufs=3))
-        qpool = ctx.enter_context(tc.tile_pool(name="quant", bufs=3))
+        epool = ctx.enter_context(tc.tile_pool(name="expo", bufs=LEAD + 5))
+        dpool = ctx.enter_context(tc.tile_pool(name="drop", bufs=6))
+        gpool = ctx.enter_context(tc.tile_pool(name="grouped", bufs=4))
+        qpool = ctx.enter_context(tc.tile_pool(name="quant", bufs=4))
         opool = ctx.enter_context(tc.tile_pool(name="outs", bufs=3))
-        spool = ctx.enter_context(tc.tile_pool(name="stats", bufs=4))
+        spool = ctx.enter_context(tc.tile_pool(name="stats", bufs=5))
         gps = ctx.enter_context(tc.psum_pool(name="gps", bufs=5))
         tps = ctx.enter_context(tc.psum_pool(name="tps", bufs=2))
         ops = ctx.enter_context(tc.psum_pool(name="ops", bufs=1))
@@ -61,9 +64,14 @@ def tile_model_kernel(tc, x1, dropout_mask, out):
         nmax = {}
         ssum = {}
         rs = {}
+        gt = {}
         et = {}
+        dd = {}
         xt = {}
         grp = {}
+        cod = {}
+        ot = {}
+        stp = {}
 
         def load(q):
             i, j = pairs[q]
@@ -73,23 +81,26 @@ def tile_model_kernel(tc, x1, dropout_mask, out):
             )
             mk[q] = m
 
-        def setup_m(j):
-            st = gps.tile([P, MT, P], BF16, tag="g", name="stm")
+        def setup_pe(r):
+            st = gps.tile([P, MT, P], BF16, tag="g", name="st")
+            src = xa if r < NG else xc
+            idx = r if r < NG else r // NG
             for t in range(MT):
-                nc.tensor.transpose(st[:, t, :], xa[:, j, t, :], ident[:])
-            nc.vector.tensor_scalar_mul(out=xtm[:, j], in0=st[:], scalar1=-1.0)
+                nc.tensor.transpose(st[:, t, :], src[:, idx, t, :], ident[:])
+            stp[r] = st
 
-        def setup_n(i):
-            st = gps.tile([P, MT, P], BF16, tag="g", name="stn")
-            for c in range(MT):
-                nc.tensor.transpose(st[:, c, :], xc[:, i, c, :], ident[:])
-            nc.scalar.copy(out=xtn[:, i], in_=st[:])
+        def setup_copy(r):
+            if r < NG:
+                nc.vector.tensor_scalar_mul(out=xtm[:, r], in0=stp[r][:], scalar1=-1.0)
+            else:
+                nc.scalar.copy(out=xtn[:, r // NG], in_=stp[r][:])
 
-        def stage_a(q, t):
+        def needs_setup(r):
+            return 0 < r < npairs and (r < NG or r % NG == 0)
+
+        def qk(k):
+            q, t = divmod(k, MT)
             i, j = pairs[q]
-            if t == 0:
-                nmax[q] = spool.tile([P, MT], F32, name="nmax")
-                ssum[q] = spool.tile([P, MT], F32, name="ssum")
             g = gps.tile([P, ROWS], F32, tag="g", name="g")
             nc.tensor.matmul(
                 out=g[:],
@@ -98,88 +109,101 @@ def tile_model_kernel(tc, x1, dropout_mask, out):
                 start=True,
                 stop=True,
             )
+            gt[k] = g
+
+        def vmin(k):
+            q, t = divmod(k, MT)
+            if t == 0:
+                nmax[q] = spool.tile([P, MT], F32, name="nmax")
+                ssum[q] = spool.tile([P, MT], F32, name="ssum")
             nc.vector.tensor_reduce(
-                out=nmax[q][:, t : t + 1], in_=g[:], axis=AX.X, op=ALU.min
+                out=nmax[q][:, t : t + 1], in_=gt[k][:], axis=AX.X, op=ALU.min
             )
+
+        def sexp(k):
+            q, t = divmod(k, MT)
             e = epool.tile([P, ROWS], F32, name="e")
             nc.scalar.activation(
                 out=e[:],
-                in_=g[:],
+                in_=gt[k][:],
                 func=ACT.Exp,
                 bias=nmax[q][:, t : t + 1],
                 scale=-1.0,
                 accum_out=ssum[q][:, t : t + 1],
             )
-            et[(q, t)] = e
+            et[k] = e
 
         def recip(q):
             rs[q] = spool.tile([P, MT], F32, name="rs")
             nc.vector.reciprocal(out=rs[q][:], in_=ssum[q][:])
 
-        def stage_b(q, t):
+        def stt(k):
+            q, t = divmod(k, MT)
             d = dpool.tile([P, ROWS], BF16, name="d")
             nc.vector.scalar_tensor_tensor(
                 out=d[:],
-                in0=et[(q, t)][:],
+                in0=et[k][:],
                 scalar=rs[q][:, t : t + 1],
                 in1=mk[q][:, t, :],
                 op0=ALU.mult,
                 op1=ALU.mult,
             )
-            h, a = divmod(t, 2)
+            dd[k] = d
+
+        def tr(k):
+            b, a = divmod(k, 2)
             if a == 0:
-                xt[(q, h)] = tps.tile([P, 2, MT, P], BF16, name="xt")
+                xt[b] = tps.tile([P, 2, MT, P], BF16, name="xt")
             for c in range(MT):
                 nc.tensor.transpose(
-                    xt[(q, h)][:, a, c, :], d[:, c * P : (c + 1) * P], ident[:]
+                    xt[b][:, a, c, :], dd[k][:, c * P : (c + 1) * P], ident[:]
                 )
 
-        def cpy(q, h):
-            if h == 0:
-                grp[q] = gpool.tile([P, ROWS, MT], BF16, name="grp", align_bytes=64)
-            nc.scalar.copy(
-                out=grp[q][:, h * 2 * P : (h + 1) * 2 * P, :].rearrange(
-                    "p (a m) c -> p a m c", a=2
-                ),
-                in_=xt[(q, h)][:].rearrange("p a c m -> p a m c"),
+        def cpy(b):
+            grp[b] = gpool.tile([P, 2, P, MT], BF16, name="grp", align_bytes=64)
+            nc.scalar.copy(out=grp[b][:], in_=xt[b][:].rearrange("p a c m -> p a m c"))
+
+        def quant_x(j):
+            nc.vector.quantize_mx(
+                out=xq[:, j * D : (j + 1) * D].bitcast(FP8X4),
+                scales=xs[:, j * D : (j + 1) * D],
+                in_=xg[:, j].rearrange("p k c -> p (k c)"),
             )
 
-        def quant_x():
-            flat = xg[:].rearrange("p j k c -> p (j k c)")
-            nc.vector.quantize_mx(
-                out=xq[:, 0:512].bitcast(FP8X4), scales=xs[:, 0:512], in_=flat[:, 0:2048]
-            )
-            nc.vector.quantize_mx(
-                out=xq[:, 512:768].bitcast(FP8X4),
-                scales=xs[:, 512:768],
-                in_=flat[:, 2048:3072],
-            )
-
-        def stage_c(q):
-            i, j = pairs[q]
-            codes = qpool.tile([P, ROWS], U32, name="codes", align_bytes=64)
-            scl = qpool.tile([P, ROWS], U8, name="scl", align_bytes=64)
+        def quant(b):
+            codes = qpool.tile([P, 2 * P], U32, name="codes", align_bytes=64)
+            scl = qpool.tile([P, 2 * P], U8, name="scl", align_bytes=64)
             nc.vector.quantize_mx(
                 out=codes[:].bitcast(FP8X4),
                 scales=scl[:],
-                in_=grp[q][:].rearrange("p m c -> p (m c)"),
+                in_=grp[b][:].rearrange("p a m c -> p (a m c)"),
             )
-            o = ops.tile([P, MT, D], F32, name="o")
-            for t in range(MT):
+            cod[b] = (codes, scl)
+
+        def mx(b):
+            q, h = divmod(b, 2)
+            i, j = pairs[q]
+            if h == 0:
+                ot[q] = ops.tile([P, MT, D], F32, name="o")
+            codes, scl = cod[b]
+            for a in range(2):
                 nc.tensor.matmul_mx(
-                    out=o[:, t, :],
-                    lhsT=codes[:, t * P : (t + 1) * P].bitcast(FP8X4),
-                    lhsT_scale=scl[:, t * P : (t + 1) * P],
+                    out=ot[q][:, 2 * h + a, :],
+                    lhsT=codes[:, a * P : (a + 1) * P].bitcast(FP8X4),
+                    lhsT_scale=scl[:, a * P : (a + 1) * P],
                     rhs=xq[:, j * D : (j + 1) * D].bitcast(FP8X4),
                     rhs_scale=xs[:, j * D : (j + 1) * D],
                     start=True,
                     stop=True,
                 )
+
+        def ocopy(q):
+            i, j = pairs[q]
             ob = opool.tile([P, MT, D], F32, name="ob")
-            if OC_V_EVERY > 0 and q % OC_V_EVERY == 0:
-                nc.vector.tensor_copy(out=ob[:], in_=o[:])
+            if OCV > 0 and q % OCV == 0:
+                nc.vector.tensor_copy(out=ob[:], in_=ot[q][:])
             else:
-                nc.scalar.copy(out=ob[:], in_=o[:])
+                nc.scalar.copy(out=ob[:], in_=ot[q][:])
             nc.sync.dma_start(
                 out=out[i, j].rearrange("(p t) k -> p t k", t=MT), in_=ob[:]
             )
@@ -190,10 +214,10 @@ def tile_model_kernel(tc, x1, dropout_mask, out):
         nc.sync.dma_start(
             out=xc[:, 0], in_=x1[0, 0].rearrange("(c p) k -> p c k", p=P)
         )
-        load(0)
         nc.sync.dma_start(
             out=xa[:, 1:], in_=x1[0, 1:].rearrange("j (p t) k -> p j t k", t=MT)
         )
+        load(0)
         nc.sync.dma_start(
             out=xc[:, 1:], in_=x1[0, 1:].rearrange("j (c p) k -> p j c k", p=P)
         )
@@ -203,41 +227,50 @@ def tile_model_kernel(tc, x1, dropout_mask, out):
         if PIN:
             ctx.enter_context(tc.manual_schedule())
 
-        setup_n(0)
-        setup_m(0)
+        st0 = gps.tile([P, MT, P], BF16, tag="g", name="st0")
         for t in range(MT):
-            stage_a(0, t)
-        nc.gpsimd.tensor_scalar(
-            out=xg[:],
-            in0=xc[:].rearrange("p j c k -> p j k c"),
-            scalar1=1.0,
-            scalar2=0.0,
-            op0=ALU.mult,
-            op1=ALU.add,
-        )
+            nc.tensor.transpose(st0[:, t, :], xc[:, 0, t, :], ident[:])
+        nc.scalar.copy(out=xtn[:, 0], in_=st0[:])
+        st1 = gps.tile([P, MT, P], BF16, tag="g", name="st1")
+        for t in range(MT):
+            nc.tensor.transpose(st1[:, t, :], xa[:, 0, t, :], ident[:])
+        nc.vector.tensor_scalar_mul(out=xtm[:, 0], in0=st1[:], scalar1=-1.0)
+        for j in range(NG):
+            nc.gpsimd.tensor_scalar(
+                out=xg[:, j],
+                in0=xc[:, j].rearrange("p c k -> p k c"),
+                scalar1=1.0,
+                scalar2=0.0,
+                op0=ALU.mult,
+                op1=ALU.add,
+            )
 
-        for q in range(npairs):
-            nq = q + 1
-            if nq < npairs:
-                ni, nj = pairs[nq]
-                if ni == 0:
-                    setup_m(nj)
-                elif nj == 0:
-                    setup_n(ni)
-            for t in range(MT):
-                if nq < npairs:
-                    stage_a(nq, t)
-                if t == 0:
-                    recip(q)
-                stage_b(q, t)
-                if t == 1:
-                    cpy(q, 0)
-                    if q == 1:
-                        quant_x()
-                    if q >= 1:
-                        stage_c(q - 1)
-                if t == 3:
-                    cpy(q, 1)
-            if q + PF < npairs:
-                load(q + PF)
-        stage_c(npairs - 1)
+        for k in range(-(LEAD + 1), ntiles + 11):
+            kq = k + LEAD + 1
+            ka = k + LEAD
+            if kq < ntiles:
+                qk(kq)
+                if kq % MT == 1 and needs_setup(kq // MT + 1):
+                    setup_pe(kq // MT + 1)
+                if kq % MT == 2 and needs_setup(kq // MT + 1):
+                    setup_copy(kq // MT + 1)
+            if (k - 7) % 2 == 0 and 0 <= (k - 7) // 2 < nbanks:
+                mx((k - 7) // 2)
+            if 0 <= ka < ntiles:
+                vmin(ka)
+                sexp(ka)
+            if 0 <= k < ntiles:
+                if k % MT == 0:
+                    recip(k // MT)
+                stt(k)
+                tr(k)
+            if (k - 10) % MT == 0 and 0 <= (k - 10) // MT < npairs:
+                ocopy((k - 10) // MT)
+            if (k - 3) % 2 == 0 and 0 <= (k - 3) // 2 < nbanks:
+                cpy((k - 3) // 2)
+            if (k - 5) % MT == 0 and 0 <= (k - 5) // MT < NG:
+                quant_x((k - 5) // MT)
+            if (k - 5) % 2 == 0 and 0 <= (k - 5) // 2 < nbanks:
+                quant((k - 5) // 2)
+            if k % MT == 3 and 0 <= k < ntiles and k // MT + PF < npairs:
+                load(k // MT + PF)

@@ -21,8 +21,10 @@ FLOPS = 2 * 2 * NG * NG * ROWS * ROWS * D
 
 PIN = True
 PF = 8
-LEAD = 6
-OCV = 0
+OCV_MOD = 2
+OCV_SET = (0,)
+G_MOD = 1
+G_TILES = ((3,),)
 
 
 def tile_model_kernel(tc, x1, dropout_mask, out):
@@ -34,7 +36,7 @@ def tile_model_kernel(tc, x1, dropout_mask, out):
     with ExitStack() as ctx:
         const = ctx.enter_context(tc.tile_pool(name="const", bufs=1))
         mpool = ctx.enter_context(tc.tile_pool(name="mask", bufs=PF))
-        epool = ctx.enter_context(tc.tile_pool(name="expo", bufs=LEAD + 5))
+        epool = ctx.enter_context(tc.tile_pool(name="expo", bufs=12))
         dpool = ctx.enter_context(tc.tile_pool(name="drop", bufs=6))
         gpool = ctx.enter_context(tc.tile_pool(name="grouped", bufs=4))
         qpool = ctx.enter_context(tc.tile_pool(name="quant", bufs=4))
@@ -160,8 +162,29 @@ def tile_model_kernel(tc, x1, dropout_mask, out):
                 )
 
         def cpy(b):
-            grp[b] = gpool.tile([P, 2, P, MT], BF16, name="grp", align_bytes=64)
-            nc.scalar.copy(out=grp[b][:], in_=xt[b][:].rearrange("p a c m -> p a m c"))
+            q, h = divmod(b, 2)
+            if h == 0:
+                grp[q] = gpool.tile([P, MT, P, MT], BF16, name="grp", align_bytes=64)
+            nc.scalar.copy(
+                out=grp[q][:, 2 * h : 2 * h + 2],
+                in_=xt[b][:].rearrange("p a c m -> p a m c"),
+            )
+
+        def gmul(k):
+            q, t = divmod(k, MT)
+            d = dpool.tile([P, ROWS], BF16, name="d")
+            nc.gpsimd.tensor_scalar(
+                out=et[k][:],
+                in0=et[k][:],
+                scalar1=rs[q][:, t : t + 1],
+                scalar2=0.0,
+                op0=ALU.mult,
+                op1=ALU.add,
+            )
+            nc.gpsimd.tensor_tensor(
+                out=d[:], in0=et[k][:], in1=mk[q][:, t, :], op=ALU.mult
+            )
+            dd[k] = d
 
         def quant_x(j):
             nc.vector.quantize_mx(
@@ -170,25 +193,23 @@ def tile_model_kernel(tc, x1, dropout_mask, out):
                 in_=xg[:, j].rearrange("p k c -> p (k c)"),
             )
 
-        def quant(b):
-            codes = qpool.tile([P, 2 * P], U32, name="codes", align_bytes=64)
-            scl = qpool.tile([P, 2 * P], U8, name="scl", align_bytes=64)
+        def quant(q):
+            codes = qpool.tile([P, ROWS], U32, name="codes", align_bytes=64)
+            scl = qpool.tile([P, ROWS], U8, name="scl", align_bytes=64)
             nc.vector.quantize_mx(
                 out=codes[:].bitcast(FP8X4),
                 scales=scl[:],
-                in_=grp[b][:].rearrange("p a m c -> p (a m c)"),
+                in_=grp[q][:].rearrange("p a m c -> p (a m c)"),
             )
-            cod[b] = (codes, scl)
+            cod[q] = (codes, scl)
 
-        def mx(b):
-            q, h = divmod(b, 2)
+        def mx(q):
             i, j = pairs[q]
-            if h == 0:
-                ot[q] = ops.tile([P, MT, D], F32, name="o")
-            codes, scl = cod[b]
-            for a in range(2):
+            ot[q] = ops.tile([P, MT, D], F32, name="o")
+            codes, scl = cod[q]
+            for a in range(MT):
                 nc.tensor.matmul_mx(
-                    out=ot[q][:, 2 * h + a, :],
+                    out=ot[q][:, a, :],
                     lhsT=codes[:, a * P : (a + 1) * P].bitcast(FP8X4),
                     lhsT_scale=scl[:, a * P : (a + 1) * P],
                     rhs=xq[:, j * D : (j + 1) * D].bitcast(FP8X4),
@@ -200,7 +221,7 @@ def tile_model_kernel(tc, x1, dropout_mask, out):
         def ocopy(q):
             i, j = pairs[q]
             ob = opool.tile([P, MT, D], F32, name="ob")
-            if OCV > 0 and q % OCV == 0:
+            if q % OCV_MOD in OCV_SET:
                 nc.vector.tensor_copy(out=ob[:], in_=ot[q][:])
             else:
                 nc.scalar.copy(out=ob[:], in_=ot[q][:])
@@ -245,32 +266,43 @@ def tile_model_kernel(tc, x1, dropout_mask, out):
                 op1=ALU.add,
             )
 
-        for k in range(-(LEAD + 1), ntiles + 11):
-            kq = k + LEAD + 1
-            ka = k + LEAD
-            if kq < ntiles:
-                qk(kq)
-                if kq % MT == 1 and needs_setup(kq // MT + 1):
-                    setup_pe(kq // MT + 1)
-                if kq % MT == 2 and needs_setup(kq // MT + 1):
-                    setup_copy(kq // MT + 1)
-            if (k - 7) % 2 == 0 and 0 <= (k - 7) // 2 < nbanks:
-                mx((k - 7) // 2)
-            if 0 <= ka < ntiles:
-                vmin(ka)
-                sexp(ka)
-            if 0 <= k < ntiles:
-                if k % MT == 0:
-                    recip(k // MT)
-                stt(k)
-                tr(k)
-            if (k - 10) % MT == 0 and 0 <= (k - 10) // MT < npairs:
-                ocopy((k - 10) // MT)
-            if (k - 3) % 2 == 0 and 0 <= (k - 3) // 2 < nbanks:
-                cpy((k - 3) // 2)
-            if (k - 5) % MT == 0 and 0 <= (k - 5) // MT < NG:
-                quant_x((k - 5) // MT)
-            if (k - 5) % 2 == 0 and 0 <= (k - 5) // 2 < nbanks:
-                quant((k - 5) // 2)
-            if k % MT == 3 and 0 <= k < ntiles and k // MT + PF < npairs:
-                load(k // MT + PF)
+
+        def on_g(k):
+            q, t = divmod(k, MT)
+            return t in G_TILES[q % G_MOD]
+
+        for p in range(-2, npairs + 4):
+            if 0 <= p < npairs:
+                recip(p)
+                for t in range(MT):
+                    if on_g(p * MT + t):
+                        gmul(p * MT + t)
+            if 0 <= p - 3 < npairs:
+                mx(p - 3)
+            if 0 <= p - 1 < npairs:
+                cpy(2 * (p - 1))
+            for t in range(MT):
+                if 0 <= p + 2 < npairs:
+                    qk((p + 2) * MT + t)
+                if 0 <= p + 1 < npairs:
+                    vmin((p + 1) * MT + t)
+                    sexp((p + 1) * MT + t)
+            if needs_setup(p + 3):
+                setup_pe(p + 3)
+            if 0 <= p - 1 < npairs:
+                cpy(2 * (p - 1) + 1)
+            if 0 <= p - 3 < npairs:
+                ocopy(p - 3)
+            if 0 <= p < npairs:
+                for t in range(MT):
+                    if not on_g(p * MT + t):
+                        stt(p * MT + t)
+                    tr(p * MT + t)
+            if 0 <= p - 2 < NG:
+                quant_x(p - 2)
+            if 0 <= p - 2 < npairs:
+                quant(p - 2)
+            if needs_setup(p + 3):
+                setup_copy(p + 3)
+            if 0 <= p < npairs and p + PF < npairs:
+                load(p + PF)

@@ -19,20 +19,13 @@ P = 128
 MT = 4
 FLOPS = 2 * 2 * NG * NG * ROWS * ROWS * D
 
-PIN = True
 PF = 8
-OCV_MOD = 2
-OCV_SET = (0,)
-G_MOD = 1
-G_TILES = ((3,),)
 
 
 def tile_model_kernel(tc, x1, dropout_mask, out):
     nc = tc.nc
     pairs = [(i, j) for i in range(NG) for j in range(NG)]
     npairs = len(pairs)
-    ntiles = npairs * MT
-    nbanks = npairs * 2
     with ExitStack() as ctx:
         const = ctx.enter_context(tc.tile_pool(name="const", bufs=1))
         mpool = ctx.enter_context(tc.tile_pool(name="mask", bufs=PF))
@@ -40,7 +33,7 @@ def tile_model_kernel(tc, x1, dropout_mask, out):
         dpool = ctx.enter_context(tc.tile_pool(name="drop", bufs=6))
         gpool = ctx.enter_context(tc.tile_pool(name="grouped", bufs=4))
         qpool = ctx.enter_context(tc.tile_pool(name="quant", bufs=4))
-        opool = ctx.enter_context(tc.tile_pool(name="outs", bufs=3))
+        opool = ctx.enter_context(tc.tile_pool(name="outs", bufs=4))
         spool = ctx.enter_context(tc.tile_pool(name="stats", bufs=5))
         gps = ctx.enter_context(tc.psum_pool(name="gps", bufs=5))
         tps = ctx.enter_context(tc.psum_pool(name="tps", bufs=2))
@@ -54,7 +47,6 @@ def tile_model_kernel(tc, x1, dropout_mask, out):
         ident = const.tile([P, P], BF16, name="ident")
         make_identity(nc, ident[:])
 
-        xa = const.tile([P, NG, MT, D], BF16, name="xa")
         xc = const.tile([P, NG, MT, D], BF16, name="xc")
         xtm = const.tile([P, NG, MT, P], BF16, name="xtm")
         xtn = const.tile([P, NG, MT, P], BF16, name="xtn")
@@ -83,108 +75,116 @@ def tile_model_kernel(tc, x1, dropout_mask, out):
             )
             mk[q] = m
 
-        def setup_pe(r):
-            st = gps.tile([P, MT, P], BF16, tag="g", name="st")
-            src = xa if r < NG else xc
-            idx = r if r < NG else r // NG
-            for t in range(MT):
-                nc.tensor.transpose(st[:, t, :], src[:, idx, t, :], ident[:])
-            stp[r] = st
+        def setup_pe(j0, n):
+            st = tps.tile([P, 2, MT, P], BF16, name="xt")
+            for a in range(n):
+                for c in range(MT):
+                    nc.tensor.transpose(st[:, a, c, :], xc[:, j0 + a, c, :], ident[:])
+            stp[j0] = st
 
-        def setup_copy(r):
-            if r < NG:
-                nc.vector.tensor_scalar_mul(out=xtm[:, r], in0=stp[r][:], scalar1=-1.0)
-            else:
-                nc.scalar.copy(out=xtn[:, r // NG], in_=stp[r][:])
+        def setup_s(j0, n):
+            nc.scalar.copy(out=xtn[:, j0 : j0 + n], in_=stp[j0][:, 0:n])
 
-        def needs_setup(r):
-            return 0 < r < npairs and (r < NG or r % NG == 0)
-
-        def qk(k):
-            q, t = divmod(k, MT)
-            i, j = pairs[q]
-            g = gps.tile([P, ROWS], F32, tag="g", name="g")
-            nc.tensor.matmul(
-                out=g[:],
-                lhsT=xtm[:, j, t, :],
-                rhs=xtn[:, i].rearrange("k c p -> k (c p)"),
-                start=True,
-                stop=True,
+        def setup_v(j):
+            nc.vector.tensor_scalar_mul(
+                out=xtm[:, j],
+                in0=xtn[:, j].rearrange("k c p -> k (c p)").rearrange(
+                    "k (p t) -> k t p", t=MT
+                ),
+                scalar1=-1.0,
             )
-            gt[k] = g
 
-        def vmin(k):
-            q, t = divmod(k, MT)
+        def setup_g(j):
+            nc.gpsimd.tensor_scalar(
+                out=xg[:, j],
+                in0=xc[:, j].rearrange("p c k -> p k c"),
+                scalar1=1.0,
+                scalar2=0.0,
+                op0=ALU.mult,
+                op1=ALU.add,
+            )
+
+        def qk(q):
+            i, j = pairs[q]
+            for t in range(MT):
+                g = gps.tile([P, ROWS], F32, tag="g", name="g")
+                nc.tensor.matmul(
+                    out=g[:],
+                    lhsT=xtm[:, j, t, :],
+                    rhs=xtn[:, i].rearrange("k c p -> k (c p)"),
+                    start=True,
+                    stop=True,
+                )
+                gt[(q, t)] = g
+
+        def vmin(q, t):
             if t == 0:
                 nmax[q] = spool.tile([P, MT], F32, name="nmax")
                 ssum[q] = spool.tile([P, MT], F32, name="ssum")
             nc.vector.tensor_reduce(
-                out=nmax[q][:, t : t + 1], in_=gt[k][:], axis=AX.X, op=ALU.min
+                out=nmax[q][:, t : t + 1], in_=gt[(q, t)][:], axis=AX.X, op=ALU.min
             )
 
-        def sexp(k):
-            q, t = divmod(k, MT)
+        def sexp(q, t):
             e = epool.tile([P, ROWS], F32, name="e")
             nc.scalar.activation(
                 out=e[:],
-                in_=gt[k][:],
+                in_=gt[(q, t)][:],
                 func=ACT.Exp,
                 bias=nmax[q][:, t : t + 1],
                 scale=-1.0,
                 accum_out=ssum[q][:, t : t + 1],
             )
-            et[k] = e
+            et[(q, t)] = e
 
         def recip(q):
             rs[q] = spool.tile([P, MT], F32, name="rs")
             nc.vector.reciprocal(out=rs[q][:], in_=ssum[q][:])
 
-        def stt(k):
-            q, t = divmod(k, MT)
+        def vmul(q, t):
             d = dpool.tile([P, ROWS], BF16, name="d")
             nc.vector.scalar_tensor_tensor(
                 out=d[:],
-                in0=et[k][:],
+                in0=et[(q, t)][:],
                 scalar=rs[q][:, t : t + 1],
                 in1=mk[q][:, t, :],
                 op0=ALU.mult,
                 op1=ALU.mult,
             )
-            dd[k] = d
+            dd[(q, t)] = d
 
-        def tr(k):
-            b, a = divmod(k, 2)
-            if a == 0:
-                xt[b] = tps.tile([P, 2, MT, P], BF16, name="xt")
-            for c in range(MT):
-                nc.tensor.transpose(
-                    xt[b][:, a, c, :], dd[k][:, c * P : (c + 1) * P], ident[:]
-                )
-
-        def cpy(b):
-            q, h = divmod(b, 2)
-            if h == 0:
-                grp[q] = gpool.tile([P, MT, P, MT], BF16, name="grp", align_bytes=64)
-            nc.scalar.copy(
-                out=grp[q][:, 2 * h : 2 * h + 2],
-                in_=xt[b][:].rearrange("p a c m -> p a m c"),
-            )
-
-        def gmul(k):
-            q, t = divmod(k, MT)
+        def gmul(q, t):
             d = dpool.tile([P, ROWS], BF16, name="d")
+            e = et[(q, t)]
             nc.gpsimd.tensor_scalar(
-                out=et[k][:],
-                in0=et[k][:],
+                out=e[:],
+                in0=e[:],
                 scalar1=rs[q][:, t : t + 1],
                 scalar2=0.0,
                 op0=ALU.mult,
                 op1=ALU.add,
             )
-            nc.gpsimd.tensor_tensor(
-                out=d[:], in0=et[k][:], in1=mk[q][:, t, :], op=ALU.mult
-            )
-            dd[k] = d
+            nc.gpsimd.tensor_tensor(out=d[:], in0=e[:], in1=mk[q][:, t, :], op=ALU.mult)
+            dd[(q, t)] = d
+
+        def tr(q, t):
+            h, a = divmod(t, 2)
+            if a == 0:
+                xt[(q, h)] = tps.tile([P, 2, MT, P], BF16, name="xt")
+            for c in range(MT):
+                nc.tensor.transpose(
+                    xt[(q, h)][:, a, c, :], dd[(q, t)][:, c * P : (c + 1) * P], ident[:]
+                )
+
+        def cpy(q, h, eng):
+            if q not in grp:
+                grp[q] = gpool.tile([P, MT, P, MT], BF16, name="grp", align_bytes=64)
+            dst = grp[q][:, 2 * h : 2 * h + 2]
+            src = xt[(q, h)][:].rearrange("p a c m -> p a m c")
+            if eng == "v":
+                nc.vector.tensor_copy(out=dst, in_=src)
+            else:
+                nc.scalar.copy(out=dst, in_=src)
 
         def quant_x(j):
             nc.vector.quantize_mx(
@@ -203,9 +203,12 @@ def tile_model_kernel(tc, x1, dropout_mask, out):
             )
             cod[q] = (codes, scl)
 
-        def mx(q):
+        def mx(q, spare):
             i, j = pairs[q]
-            ot[q] = ops.tile([P, MT, D], F32, name="o")
+            if spare:
+                ot[q] = gps.tile([P, MT, D], F32, tag="g", name="og")
+            else:
+                ot[q] = ops.tile([P, MT, D], F32, name="o")
             codes, scl = cod[q]
             for a in range(MT):
                 nc.tensor.matmul_mx(
@@ -218,10 +221,10 @@ def tile_model_kernel(tc, x1, dropout_mask, out):
                     stop=True,
                 )
 
-        def ocopy(q):
+        def ocopy(q, eng):
             i, j = pairs[q]
             ob = opool.tile([P, MT, D], F32, name="ob")
-            if q % OCV_MOD in OCV_SET:
+            if eng == "v":
                 nc.vector.tensor_copy(out=ob[:], in_=ot[q][:])
             else:
                 nc.scalar.copy(out=ob[:], in_=ot[q][:])
@@ -230,79 +233,85 @@ def tile_model_kernel(tc, x1, dropout_mask, out):
             )
 
         nc.sync.dma_start(
-            out=xa[:, 0], in_=x1[0, 0].rearrange("(p t) k -> p t k", t=MT)
-        )
-        nc.sync.dma_start(
             out=xc[:, 0], in_=x1[0, 0].rearrange("(c p) k -> p c k", p=P)
         )
         nc.sync.dma_start(
-            out=xa[:, 1:], in_=x1[0, 1:].rearrange("j (p t) k -> p j t k", t=MT)
-        )
-        load(0)
-        nc.sync.dma_start(
             out=xc[:, 1:], in_=x1[0, 1:].rearrange("j (c p) k -> p j c k", p=P)
         )
-        for q in range(1, PF):
+        for q in range(PF):
             load(q)
 
-        if PIN:
-            ctx.enter_context(tc.manual_schedule())
+        ctx.enter_context(tc.manual_schedule())
 
-        st0 = gps.tile([P, MT, P], BF16, tag="g", name="st0")
-        for t in range(MT):
-            nc.tensor.transpose(st0[:, t, :], xc[:, 0, t, :], ident[:])
-        nc.scalar.copy(out=xtn[:, 0], in_=st0[:])
-        st1 = gps.tile([P, MT, P], BF16, tag="g", name="st1")
-        for t in range(MT):
-            nc.tensor.transpose(st1[:, t, :], xa[:, 0, t, :], ident[:])
-        nc.vector.tensor_scalar_mul(out=xtm[:, 0], in0=st1[:], scalar1=-1.0)
+        setup_pe(0, 1)
+        setup_s(0, 1)
+        setup_v(0)
         for j in range(NG):
-            nc.gpsimd.tensor_scalar(
-                out=xg[:, j],
-                in0=xc[:, j].rearrange("p c k -> p k c"),
-                scalar1=1.0,
-                scalar2=0.0,
-                op0=ALU.mult,
-                op1=ALU.add,
-            )
+            setup_g(j)
+        qk(0)
+        setup_pe(1, 1)
+        vmin(0, 0)
+        sexp(0, 0)
+        setup_s(1, 1)
+        for t in range(1, MT):
+            vmin(0, t)
+            sexp(0, t)
+        setup_v(1)
+        qk(1)
+        setup_pe(2, 2)
+        setup_s(2, 2)
+        setup_pe(4, 2)
 
-
-        def on_g(k):
-            q, t = divmod(k, MT)
-            return t in G_TILES[q % G_MOD]
-
-        for p in range(-2, npairs + 4):
-            if 0 <= p < npairs:
+        last = npairs - 1
+        for p in range(last):
+            if p > 0:
                 recip(p)
-                for t in range(MT):
-                    if on_g(p * MT + t):
-                        gmul(p * MT + t)
-            if 0 <= p - 3 < npairs:
-                mx(p - 3)
-            if 0 <= p - 1 < npairs:
-                cpy(2 * (p - 1))
+                gmul(p, 3)
+            if p >= 3:
+                mx(p - 3, False)
+            if p >= 1:
+                cpy(p - 1, 0, "s")
             for t in range(MT):
-                if 0 <= p + 2 < npairs:
-                    qk((p + 2) * MT + t)
-                if 0 <= p + 1 < npairs:
-                    vmin((p + 1) * MT + t)
-                    sexp((p + 1) * MT + t)
-            if needs_setup(p + 3):
-                setup_pe(p + 3)
-            if 0 <= p - 1 < npairs:
-                cpy(2 * (p - 1) + 1)
-            if 0 <= p - 3 < npairs:
-                ocopy(p - 3)
-            if 0 <= p < npairs:
-                for t in range(MT):
-                    if not on_g(p * MT + t):
-                        stt(p * MT + t)
-                    tr(p * MT + t)
+                vmin(p + 1, t)
+                sexp(p + 1, t)
+            if p == 0:
+                recip(p)
+                setup_s(4, 2)
+            if p + 2 < NG:
+                setup_v(p + 2)
+            if p + 2 < npairs:
+                qk(p + 2)
+            if p >= 1:
+                cpy(p - 1, 1, "s")
+            if p >= 3:
+                ocopy(p - 3, "v" if p % 2 == 1 else "s")
+            for t in range(MT):
+                if t < 3 or p == 0:
+                    vmul(p, t)
+                tr(p, t)
             if 0 <= p - 2 < NG:
                 quant_x(p - 2)
-            if 0 <= p - 2 < npairs:
+            if p >= 2:
                 quant(p - 2)
-            if needs_setup(p + 3):
-                setup_copy(p + 3)
-            if 0 <= p < npairs and p + PF < npairs:
+            if p + PF < npairs:
                 load(p + PF)
+
+        recip(last)
+        mx(last - 3, False)
+        cpy(last - 1, 0, "s")
+        for t in range(MT):
+            vmul(last, t)
+            tr(last, t)
+        cpy(last - 1, 1, "s")
+        quant(last - 2)
+        mx(last - 2, True)
+        ocopy(last - 3, "s")
+        cpy(last, 0, "s")
+        quant(last - 1)
+        mx(last - 1, True)
+        cpy(last, 1, "v")
+        ocopy(last - 2, "s")
+        quant(last)
+        mx(last, True)
+        ocopy(last - 1, "s")
+        ocopy(last, "v")

@@ -35,7 +35,7 @@ def tile_model_kernel(tc, x1, dropout_mask, out):
         qpool = ctx.enter_context(tc.tile_pool(name="quant", bufs=4))
         opool = ctx.enter_context(tc.tile_pool(name="outs", bufs=4))
         spool = ctx.enter_context(tc.tile_pool(name="stats", bufs=5))
-        gps = ctx.enter_context(tc.psum_pool(name="gps", bufs=5))
+        gps = ctx.enter_context(tc.psum_pool(name="gps", bufs=4))
         tps = ctx.enter_context(tc.psum_pool(name="tps", bufs=2))
         ops = ctx.enter_context(tc.psum_pool(name="ops", bufs=1))
 
@@ -66,6 +66,7 @@ def tile_model_kernel(tc, x1, dropout_mask, out):
         cod = {}
         ot = {}
         stp = {}
+        osb = {}
 
         def load(q):
             i, j = pairs[q]
@@ -206,13 +207,19 @@ def tile_model_kernel(tc, x1, dropout_mask, out):
         def mx(q, spare):
             i, j = pairs[q]
             if spare:
-                ot[q] = gps.tile([P, MT, D], F32, tag="g", name="og")
+                ot[q] = (
+                    gps.tile([P, 2, D], F32, tag="g", name="oga"),
+                    gps.tile([P, 2, D], F32, tag="g", name="ogb"),
+                )
             else:
-                ot[q] = ops.tile([P, MT, D], F32, name="o")
+                ot[q] = (
+                    ops.tile([P, 2, D], F32, name="oa"),
+                    ops.tile([P, 2, D], F32, name="ob2"),
+                )
             codes, scl = cod[q]
             for a in range(MT):
                 nc.tensor.matmul_mx(
-                    out=ot[q][:, a, :],
+                    out=ot[q][a // 2][:, a % 2, :],
                     lhsT=codes[:, a * P : (a + 1) * P].bitcast(FP8X4),
                     lhsT_scale=scl[:, a * P : (a + 1) * P],
                     rhs=xq[:, j * D : (j + 1) * D].bitcast(FP8X4),
@@ -221,15 +228,15 @@ def tile_model_kernel(tc, x1, dropout_mask, out):
                     stop=True,
                 )
 
-        def ocopy(q, eng):
+        def ocopy_v(q):
+            osb[q] = opool.tile([P, MT, D], F32, name="ob")
+            nc.vector.tensor_copy(out=osb[q][:, 0:2], in_=ot[q][0][:])
+
+        def ocopy_s(q):
             i, j = pairs[q]
-            ob = opool.tile([P, MT, D], F32, name="ob")
-            if eng == "v":
-                nc.vector.tensor_copy(out=ob[:], in_=ot[q][:])
-            else:
-                nc.scalar.copy(out=ob[:], in_=ot[q][:])
+            nc.scalar.copy(out=osb[q][:, 2:4], in_=ot[q][1][:])
             nc.sync.dma_start(
-                out=out[i, j].rearrange("(p t) k -> p t k", t=MT), in_=ob[:]
+                out=out[i, j].rearrange("(p t) k -> p t k", t=MT), in_=osb[q][:]
             )
 
         nc.sync.dma_start(
@@ -281,10 +288,12 @@ def tile_model_kernel(tc, x1, dropout_mask, out):
                 setup_v(p + 2)
             if p + 2 < npairs:
                 qk(p + 2)
+            if p >= 3:
+                ocopy_v(p - 3)
             if p >= 1:
                 cpy(p - 1, 1, "s")
             if p >= 3:
-                ocopy(p - 3, "v" if p % 2 == 1 else "s")
+                ocopy_s(p - 3)
             for t in range(MT):
                 if t < 3 or p == 0:
                     vmul(p, t)
@@ -305,13 +314,17 @@ def tile_model_kernel(tc, x1, dropout_mask, out):
         cpy(last - 1, 1, "s")
         quant(last - 2)
         mx(last - 2, True)
-        ocopy(last - 3, "s")
+        ocopy_v(last - 3)
+        ocopy_s(last - 3)
         cpy(last, 0, "s")
         quant(last - 1)
         mx(last - 1, True)
         cpy(last, 1, "v")
-        ocopy(last - 2, "s")
+        ocopy_v(last - 2)
+        ocopy_s(last - 2)
         quant(last)
-        mx(last, True)
-        ocopy(last - 1, "s")
-        ocopy(last, "v")
+        mx(last, False)
+        ocopy_v(last - 1)
+        ocopy_s(last - 1)
+        ocopy_v(last)
+        ocopy_s(last)

@@ -157,15 +157,15 @@ def tile_model_kernel(tc, x1, dropout_mask, out):
         def gmul(q, t):
             d = dpool.tile([P, ROWS], BF16, name="d")
             e = et[(q, t)]
+            nc.gpsimd.tensor_tensor(out=e[:], in0=e[:], in1=mk[q][:, t, :], op=ALU.mult)
             nc.gpsimd.tensor_scalar(
-                out=e[:],
+                out=d[:],
                 in0=e[:],
                 scalar1=rs[q][:, t : t + 1],
                 scalar2=0.0,
                 op0=ALU.mult,
                 op1=ALU.add,
             )
-            nc.gpsimd.tensor_tensor(out=d[:], in0=e[:], in1=mk[q][:, t, :], op=ALU.mult)
             dd[(q, t)] = d
 
         def tr(q, t):

@@ -248,7 +248,6 @@ def tile_model_kernel(tc, x1, dropout_mask, out):
         for q in range(PF):
             load(q)
 
-        ctx.enter_context(tc.manual_schedule())
 
         setup_pe(0, 1)
         setup_s(0, 1)

from contextlib import ExitStack

import concourse.mybir as mybir
from concourse.masks import make_identity

F32 = mybir.dt.float32
BF16 = mybir.dt.bfloat16
U32 = mybir.dt.uint32
U8 = mybir.dt.uint8
FP8X4 = mybir.dt.float8_e4m3fn_x4
ACT = mybir.ActivationFunctionType
ALU = mybir.AluOpType
AX = mybir.AxisListType

NG = 6
ROWS = 512
D = 128
P = 128
MT = 4
FLOPS = 2 * 2 * NG * NG * ROWS * ROWS * D

PF = 8


def tile_model_kernel(tc, x1, dropout_mask, out):
    nc = tc.nc
    pairs = [(i, j) for i in range(NG) for j in range(NG)]
    npairs = len(pairs)
    with ExitStack() as ctx:
        const = ctx.enter_context(tc.tile_pool(name="const", bufs=1))
        mpool = ctx.enter_context(tc.tile_pool(name="mask", bufs=PF))
        epool = ctx.enter_context(tc.tile_pool(name="expo", bufs=12))
        dpool = ctx.enter_context(tc.tile_pool(name="drop", bufs=6))
        gpool = ctx.enter_context(tc.tile_pool(name="grouped", bufs=4))
        qpool = ctx.enter_context(tc.tile_pool(name="quant", bufs=4))
        opool = ctx.enter_context(tc.tile_pool(name="outs", bufs=4))
        spool = ctx.enter_context(tc.tile_pool(name="stats", bufs=5))
        gps = ctx.enter_context(tc.psum_pool(name="gps", bufs=4))
        tps = ctx.enter_context(tc.psum_pool(name="tps", bufs=2))
        ops = ctx.enter_context(tc.psum_pool(name="ops", bufs=1))

        warm = const.tile([P, 1], F32, name="warm")
        warm2 = const.tile([P, 1], F32, name="warm2")
        nc.vector.memset(warm[:], 0.0)
        nc.scalar.activation(out=warm2[:], in_=warm[:], func=ACT.Exp)

        ident = const.tile([P, P], BF16, name="ident")
        make_identity(nc, ident[:])

        xc = const.tile([P, NG, MT, D], BF16, name="xc")
        xtm = const.tile([P, NG, MT, P], BF16, name="xtm")
        xtn = const.tile([P, NG, MT, P], BF16, name="xtn")
        xg = const.tile([P, NG, D, MT], BF16, name="xg", align_bytes=64)
        xq = const.tile([P, NG * D], U32, name="xq", align_bytes=64)
        xs = const.tile([P, NG * D], U8, name="xs", align_bytes=64)

        mk = {}
        nmax = {}
        ssum = {}
        rs = {}
        gt = {}
        et = {}
        dd = {}
        xt = {}
        grp = {}
        cod = {}
        ot = {}
        stp = {}
        osb = {}

        def load(q):
            i, j = pairs[q]
            m = mpool.tile([P, MT, ROWS], BF16, name="mk")
            nc.sync.dma_start(
                out=m[:], in_=dropout_mask[i, j].rearrange("(p t) n -> p t n", t=MT)
            )
            mk[q] = m

        def setup_pe(j0, n):
            st = tps.tile([P, 2, MT, P], BF16, name="xt")
            for a in range(n):
                for c in range(MT):
                    nc.tensor.transpose(st[:, a, c, :], xc[:, j0 + a, c, :], ident[:])
            stp[j0] = st

        def setup_s(j0, n):
            nc.scalar.copy(out=xtn[:, j0 : j0 + n], in_=stp[j0][:, 0:n])

        def setup_v(j):
            nc.vector.tensor_scalar_mul(
                out=xtm[:, j],
                in0=xtn[:, j].rearrange("k c p -> k (c p)").rearrange(
                    "k (p t) -> k t p", t=MT
                ),
                scalar1=-1.0,
            )

        def setup_g(j):
            nc.gpsimd.tensor_scalar(
                out=xg[:, j],
                in0=xc[:, j].rearrange("p c k -> p k c"),
                scalar1=1.0,
                scalar2=0.0,
                op0=ALU.mult,
                op1=ALU.add,
            )

        def qk(q):
            i, j = pairs[q]
            for t in range(MT):
                g = gps.tile([P, ROWS], F32, tag="g", name="g")
                nc.tensor.matmul(
                    out=g[:],
                    lhsT=xtm[:, j, t, :],
                    rhs=xtn[:, i].rearrange("k c p -> k (c p)"),
                    start=True,
                    stop=True,
                )
                gt[(q, t)] = g

        def vmin(q, t):
            if t == 0:
                nmax[q] = spool.tile([P, MT], F32, name="nmax")
                ssum[q] = spool.tile([P, MT], F32, name="ssum")
            nc.vector.tensor_reduce(
                out=nmax[q][:, t : t + 1], in_=gt[(q, t)][:], axis=AX.X, op=ALU.min
            )

        def sexp(q, t):
            e = epool.tile([P, ROWS], F32, name="e")
            nc.scalar.activation(
                out=e[:],
                in_=gt[(q, t)][:],
                func=ACT.Exp,
                bias=nmax[q][:, t : t + 1],
                scale=-1.0,
                accum_out=ssum[q][:, t : t + 1],
            )
            et[(q, t)] = e

        def recip(q):
            rs[q] = spool.tile([P, MT], F32, name="rs")
            nc.vector.reciprocal(out=rs[q][:], in_=ssum[q][:])

        def vmul(q, t):
            d = dpool.tile([P, ROWS], BF16, name="d")
            nc.vector.scalar_tensor_tensor(
                out=d[:],
                in0=et[(q, t)][:],
                scalar=rs[q][:, t : t + 1],
                in1=mk[q][:, t, :],
                op0=ALU.mult,
                op1=ALU.mult,
            )
            dd[(q, t)] = d

        def gmul(q, t):
            d = dpool.tile([P, ROWS], BF16, name="d")
            e = et[(q, t)]
            nc.gpsimd.tensor_tensor(out=e[:], in0=e[:], in1=mk[q][:, t, :], op=ALU.mult)
            nc.gpsimd.tensor_scalar(
                out=d[:],
                in0=e[:],
                scalar1=rs[q][:, t : t + 1],
                scalar2=0.0,
                op0=ALU.mult,
                op1=ALU.add,
            )
            dd[(q, t)] = d

        def tr(q, t):
            h, a = divmod(t, 2)
            if a == 0:
                xt[(q, h)] = tps.tile([P, 2, MT, P], BF16, name="xt")
            for c in range(MT):
                nc.tensor.transpose(
                    xt[(q, h)][:, a, c, :], dd[(q, t)][:, c * P : (c + 1) * P], ident[:]
                )

        def cpy(q, h, eng):
            if q not in grp:
                grp[q] = gpool.tile([P, MT, P, MT], BF16, name="grp", align_bytes=64)
            dst = grp[q][:, 2 * h : 2 * h + 2]
            src = xt[(q, h)][:].rearrange("p a c m -> p a m c")
            if eng == "v":
                nc.vector.tensor_copy(out=dst, in_=src)
            else:
                nc.scalar.copy(out=dst, in_=src)

        def quant_x(j):
            nc.vector.quantize_mx(
                out=xq[:, j * D : (j + 1) * D].bitcast(FP8X4),
                scales=xs[:, j * D : (j + 1) * D],
                in_=xg[:, j].rearrange("p k c -> p (k c)"),
            )

        def quant(q):
            codes = qpool.tile([P, ROWS], U32, name="codes", align_bytes=64)
            scl = qpool.tile([P, ROWS], U8, name="scl", align_bytes=64)
            nc.vector.quantize_mx(
                out=codes[:].bitcast(FP8X4),
                scales=scl[:],
                in_=grp[q][:].rearrange("p a m c -> p (a m c)"),
            )
            cod[q] = (codes, scl)

        def mx(q, spare):
            i, j = pairs[q]
            if spare:
                ot[q] = (
                    gps.tile([P, 2, D], F32, tag="g", name="oga"),
                    gps.tile([P, 2, D], F32, tag="g", name="ogb"),
                )
            else:
                ot[q] = (
                    ops.tile([P, 2, D], F32, name="oa"),
                    ops.tile([P, 2, D], F32, name="ob2"),
                )
            codes, scl = cod[q]
            for a in range(MT):
                nc.tensor.matmul_mx(
                    out=ot[q][a // 2][:, a % 2, :],
                    lhsT=codes[:, a * P : (a + 1) * P].bitcast(FP8X4),
                    lhsT_scale=scl[:, a * P : (a + 1) * P],
                    rhs=xq[:, j * D : (j + 1) * D].bitcast(FP8X4),
                    rhs_scale=xs[:, j * D : (j + 1) * D],
                    start=True,
                    stop=True,
                )

        def ocopy_v(q):
            osb[q] = opool.tile([P, MT, D], F32, name="ob")
            nc.vector.tensor_copy(out=osb[q][:, 0:2], in_=ot[q][0][:])

        def ocopy_s(q):
            i, j = pairs[q]
            nc.scalar.copy(out=osb[q][:, 2:4], in_=ot[q][1][:])
            nc.sync.dma_start(
                out=out[i, j].rearrange("(p t) k -> p t k", t=MT), in_=osb[q][:]
            )

        nc.sync.dma_start(
            out=xc[:, 0], in_=x1[0, 0].rearrange("(c p) k -> p c k", p=P)
        )
        nc.sync.dma_start(
            out=xc[:, 1:], in_=x1[0, 1:].rearrange("j (c p) k -> p j c k", p=P)
        )
        for q in range(PF):
            load(q)


        setup_pe(0, 1)
        setup_s(0, 1)
        setup_v(0)
        for j in range(NG):
            setup_g(j)
        qk(0)
        setup_pe(1, 1)
        vmin(0, 0)
        sexp(0, 0)
        setup_s(1, 1)
        for t in range(1, MT):
            vmin(0, t)
            sexp(0, t)
        setup_v(1)
        qk(1)
        setup_pe(2, 2)
        setup_s(2, 2)
        setup_pe(4, 2)

        last = npairs - 1
        for p in range(last):
            if p > 0:
                recip(p)
                gmul(p, 3)
            if p >= 3:
                mx(p - 3, False)
            if p >= 1:
                cpy(p - 1, 0, "s")
            for t in range(MT):
                vmin(p + 1, t)
                sexp(p + 1, t)
            if p == 0:
                recip(p)
                setup_s(4, 2)
            if p + 2 < NG:
                setup_v(p + 2)
            if p + 2 < npairs:
                qk(p + 2)
            if p >= 3:
                ocopy_v(p - 3)
            if p >= 1:
                cpy(p - 1, 1, "s")
            if p >= 3:
                ocopy_s(p - 3)
            for t in range(MT):
                if t < 3 or p == 0:
                    vmul(p, t)
                tr(p, t)
            if 0 <= p - 2 < NG:
                quant_x(p - 2)
            if p >= 2:
                quant(p - 2)
            if p + PF < npairs:
                load(p + PF)

        recip(last)
        mx(last - 3, False)
        cpy(last - 1, 0, "s")
        for t in range(MT):
            vmul(last, t)
            tr(last, t)
        cpy(last - 1, 1, "s")
        quant(last - 2)
        mx(last - 2, True)
        ocopy_v(last - 3)
        ocopy_s(last - 3)
        cpy(last, 0, "s")
        quant(last - 1)
        mx(last - 1, True)
        cpy(last, 1, "v")
        ocopy_v(last - 2)
        ocopy_s(last - 2)
        quant(last)
        mx(last, False)
        ocopy_v(last - 1)
        ocopy_s(last - 1)
        ocopy_v(last)
        ocopy_s(last)
